import numpy as np
import ml_dtypes


def mxq(x, axis, fmt="e4m3"):
    dtype, down = {"e4m3": (ml_dtypes.float8_e4m3fn, 7), "e5m2": (ml_dtypes.float8_e5m2, 14)}[fmt]
    v = np.moveaxis(np.asarray(x, np.float32).astype(ml_dtypes.bfloat16).astype(np.float64), axis, -1)
    blocks = v.reshape(v.shape[:-1] + (-1, 32))
    amax = np.abs(blocks).max(-1, keepdims=True)
    byte = np.maximum(np.where(amax > 0, np.frexp(amax)[1] - 1 + 127, 0) - down, 1)
    scale = np.exp2(byte - 127.0)
    codes = (blocks / scale).astype(np.float32).astype(dtype).astype(np.float64)
    return np.moveaxis((codes * scale).reshape(v.shape), -1, axis)


WIDE = False


def mx_kscale(k):
    if not WIDE:
        return np.ones(k)
    levels = np.array([20, -20, 10, -10, 0])
    a = np.random.permutation(np.resize(levels, k // 512 * 4)).reshape(k // 512, 4)
    idx = np.arange(k)
    return np.exp2(a[idx // 512, idx % 128 // 32])


BF16 = ml_dtypes.bfloat16


def bf(x):
    return np.asarray(x, np.float32).astype(BF16)


def f64(x):
    return np.asarray(x).astype(np.float64)


N, DIN, DOUT = 4096, 1024, 1024
MIN_NORM = 1e-15
EPS_PROJ = 4e-3
MAXNORM = 1.0 - EPS_PROJ


def rsum(v):
    return np.sum(v, axis=-1, keepdims=True)


def safe_norm(v):
    return np.sqrt(np.maximum(rsum(v * v), MIN_NORM))


def artanh(u):
    u = np.clip(u, -1.0 + 1e-5, 1.0 - 1e-5)
    return 0.5 * np.log((1.0 + u) / (1.0 - u))


def project(v):
    norm = safe_norm(v)
    return np.where(norm > MAXNORM, v / norm * MAXNORM, v)


def project_bwd(v, g):
    norm = safe_norm(v)
    return np.where(norm > MAXNORM, (g - v * rsum(g * v) / (norm * norm)) * (MAXNORM / norm), g)


def expmap0(u):
    u_norm = safe_norm(u)
    return np.tanh(u_norm) * u / u_norm


def mobius_add(x, y):
    x2 = rsum(x * x)
    y2 = rsum(y * y)
    xy = rsum(x * y)
    num = (1.0 + 2.0 * xy + y2) * x + (1.0 - x2) * y
    denom = 1.0 + 2.0 * xy + x2 * y2
    return num / np.maximum(denom, MIN_NORM)


def setup_inputs():
    s = mx_kscale(N)[:, None]
    lim = 2.0 * np.sqrt(6.0 / (DIN + DOUT))
    m = np.random.standard_normal(DIN)
    g = np.random.standard_normal((N, DIN)) + 0.5 * m
    r = 0.3 + 0.68 * np.random.random_sample((N, 1))
    w0 = np.random.uniform(-lim, lim, (DOUT, DIN))
    wm = w0 @ m
    b = wm / np.linalg.norm(wm) + np.random.standard_normal(DOUT) / np.sqrt(DOUT)
    x0 = bf(g / np.linalg.norm(g, axis=-1, keepdims=True) * r)
    weight = bf(w0)
    bias = bf(0.35 * b)
    go = bf(16.0 * np.random.standard_normal((N, DOUT)) * np.exp2(np.random.randint(-12, 1, (N, 1))) / s)
    z = f64(x0) @ f64(weight).T
    xn = safe_norm(f64(x0))
    ratio = artanh(xn) / xn
    return {"x": bf(f64(x0) * s), "weight": weight, "bias": bias,
            "z": np.asarray(z, np.float32), "ratio": np.asarray(ratio, np.float32), "grad_out": go}


def reference(x, weight, bias, z, ratio, grad_out):
    m = f64(z)
    a = f64(ratio)
    g = f64(grad_out)
    n = safe_norm(m)
    e = m / n
    t = np.tanh(n * a)
    u = t * e
    p = project(u)
    hb = project(expmap0(f64(bias)[None, :]))
    x2 = rsum(p * p)
    y2 = rsum(hb * hb)
    xy = rsum(p * hb)
    ca = 1.0 + 2.0 * xy + y2
    cb = 1.0 - x2
    den = np.maximum(1.0 + 2.0 * xy + x2 * y2, MIN_NORM)
    v = (ca * p + cb * hb) / den
    dv = project_bwd(v, g)
    q = dv / den
    dden = -rsum(q * v)
    dca = rsum(q * p)
    dcb = rsum(q * hb)
    dp = ca * q + 2.0 * (dca + dden) * hb + 2.0 * (y2 * dden - dcb) * p
    du = project_bwd(u, dp)
    ed = rsum(e * du)
    dz = (t / n) * (du - e * ed) + a * (1.0 - t * t) * ed * e
    dz = np.where(np.all(m == 0, axis=-1, keepdims=True), 0.0, dz)
    return mxq(dz, 0, "e5m2").T @ mxq(f64(x), 0, "e4m3")

@@ -1,0 +1,306 @@
+import concourse.mybir as mybir
+
+F32 = mybir.dt.float32
+BF16 = mybir.dt.bfloat16
+U32 = mybir.dt.uint32
+U8 = mybir.dt.uint8
+E4M3X4 = mybir.dt.float8_e4m3fn_x4
+E5M2X4 = mybir.dt.float8_e5m2_x4
+ALU = mybir.AluOpType
+FUNC = mybir.ActivationFunctionType
+
+P = 128
+PACK = 4
+K_PASS = P * PACK
+TOKENS = 4096
+D_IN = 1024
+D_OUT = 1024
+CHUNKS = TOKENS // K_PASS
+ROWS = CHUNKS * PACK
+BATCHES = 2
+BATCH_ROWS = ROWS // BATCHES
+N_TILE = 512
+M_TILE = 128
+SWEEP = 512
+MAXNORM = 1.0 - 4e-3
+MIN_NORM = 1e-15
+TINY = 1e-30
+
+FLOPS = 2 * TOKENS * D_IN * D_OUT
+BYTES = TOKENS * D_IN * 2 + TOKENS * D_OUT * (4 + 2) + TOKENS * 4 + D_OUT * 2 + D_OUT * D_IN * 4
+
+
+def tile_hyplinear_v_kernel(tc, x, weight, bias, z, ratio, grad_out, out):
+    nc = tc.nc
+    x_chunks = x.rearrange("(c p j) w -> c p j w", p=P, j=PACK)
+    z_chunks = z.rearrange("(c p j) w -> c p j w", p=P, j=PACK)
+    g_chunks = grad_out.rearrange("(c p j) w -> c p j w", p=P, j=PACK)
+
+    def mul(o, a, b):
+        nc.vector.tensor_tensor(out=o, in0=a, in1=b, op=ALU.mult)
+
+    def add(o, a, b):
+        nc.vector.tensor_tensor(out=o, in0=a, in1=b, op=ALU.add)
+
+    def sub(o, a, b):
+        nc.vector.tensor_tensor(out=o, in0=a, in1=b, op=ALU.subtract)
+
+    def affine(o, a, m, b):
+        nc.vector.tensor_scalar(out=o, in0=a, scalar1=m, scalar2=b, op0=ALU.mult, op1=ALU.add)
+
+    def with_const(o, a, c, op):
+        nc.vector.tensor_scalar(out=o, in0=a, scalar1=c, scalar2=None, op0=op)
+
+    def scaled_plus(o, a, m, b, op1=ALU.add):
+        nc.vector.scalar_tensor_tensor(out=o, in0=a, scalar=m, in1=b, op0=ALU.mult, op1=op1)
+
+    def dot(acc, junk, a, b):
+        nc.vector.scalar_tensor_tensor(
+            out=junk, in0=a, scalar=1.0, in1=b, op0=ALU.mult, op1=ALU.mult, accum_out=acc
+        )
+
+    with tc.tile_pool(name="keep", bufs=1) as keep, tc.tile_pool(name="small", bufs=1) as small:
+        g_all = keep.tile([P, CHUNKS, PACK, D_OUT], BF16)
+        x_codes = keep.tile([P, CHUNKS, D_IN], U32, align_bytes=64)
+        x_scales = keep.tile([P, CHUNKS, D_IN], U8, align_bytes=64)
+        hb = keep.tile([P, D_OUT], F32)
+        ratio_rows = keep.tile([P, ROWS], F32)
+        sum_zz = keep.tile([P, ROWS], F32)
+        sum_zh = keep.tile([P, ROWS], F32)
+        sum_gz = keep.tile([P, ROWS], F32)
+        sum_gh = keep.tile([P, ROWS], F32)
+        alpha = keep.tile([P, ROWS], F32)
+        beta = keep.tile([P, ROWS], F32)
+        gamma = keep.tile([P, ROWS], F32)
+        y2 = keep.tile([P, 1], F32)
+        one_plus_y2 = keep.tile([P, 1], F32)
+
+        def row_scalars(batch):
+            rows = slice(batch * BATCH_ROWS, (batch + 1) * BATCH_ROWS)
+
+            def new(name):
+                fresh = small.tile([P, BATCH_ROWS], F32, name=name)
+                return fresh[:]
+
+            n = new("n")
+            with_const(n, sum_zz[:, rows], MIN_NORM, ALU.max)
+            nc.scalar.sqrt(n, n)
+            rn = new("rn")
+            nc.vector.reciprocal(out=rn, in_=n)
+            t = new("t")
+            mul(t, n, ratio_rows[:, rows])
+            nc.scalar.activation(out=t, in_=t, func=FUNC.Tanh)
+            s = new("s")
+            with_const(s, t, MAXNORM, ALU.min)
+            he = new("he")
+            mul(he, sum_zh[:, rows], rn)
+            xy = new("xy")
+            mul(xy, s, he)
+            x2 = new("x2")
+            mul(x2, s, s)
+            ca = new("ca")
+            affine(ca, xy, 2.0, one_plus_y2[:, 0:1])
+            cb = new("cb")
+            affine(cb, x2, -1.0, 1.0)
+            den = new("den")
+            affine(den, x2, y2[:, 0:1], 1.0)
+            scaled_plus(den, xy, 2.0, den)
+            with_const(den, den, MIN_NORM, ALU.max)
+            rden = new("rden")
+            nc.vector.reciprocal(out=rden, in_=den)
+            cas = new("cas")
+            mul(cas, ca, s)
+            ve = new("ve")
+            mul(ve, cb, he)
+            add(ve, ve, cas)
+            vh = new("vh")
+            mul(vh, cas, he)
+            scaled_plus(vh, cb, y2[:, 0:1], vh)
+            vv = new("vv")
+            tmp = new("tmp")
+            mul(vv, cas, ve)
+            mul(tmp, cb, vh)
+            add(vv, vv, tmp)
+            nv = new("nv")
+            mul(nv, rden, rden)
+            mul(nv, nv, vv)
+            with_const(nv, nv, MIN_NORM, ALU.max)
+            nc.scalar.sqrt(nv, nv)
+            v_out = new("v_out")
+            with_const(v_out, nv, MAXNORM, ALU.is_gt)
+            fac = new("fac")
+            with_const(fac, nv, MAXNORM, ALU.max)
+            nc.vector.reciprocal(out=fac, in_=fac)
+            scaled_plus(fac, rden, MAXNORM, fac, op1=ALU.mult)
+            rvv = new("rvv")
+            with_const(rvv, vv, TINY, ALU.max)
+            nc.vector.reciprocal(out=rvv, in_=rvv)
+            mul(rvv, rvv, v_out)
+            ge = new("ge")
+            mul(ge, sum_gz[:, rows], rn)
+            gh = sum_gh[:, rows]
+            mu = new("mu")
+            mul(mu, cas, ge)
+            mul(tmp, cb, gh)
+            add(mu, mu, tmp)
+            mul(mu, mu, rvv)
+            qe = new("qe")
+            mul(qe, mu, ve)
+            sub(qe, ge, qe)
+            qh = new("qh")
+            mul(qh, mu, vh)
+            sub(qh, gh, qh)
+            qv = new("qv")
+            mul(qv, cas, qe)
+            mul(tmp, cb, qh)
+            add(qv, qv, tmp)
+            mul(qv, qv, rden)
+            half_ch = new("half_ch")
+            mul(half_ch, s, qe)
+            sub(half_ch, half_ch, qv)
+            half_cp = new("half_cp")
+            scaled_plus(half_cp, qv, y2[:, 0:1], qh)
+            mua = new("mua")
+            mul(mua, mu, ca)
+            dp_h = new("dp_h")
+            mul(dp_h, mua, cb)
+            scaled_plus(dp_h, half_ch, 2.0, dp_h, op1=ALU.subtract)
+            dp_e = new("dp_e")
+            mul(dp_e, mua, ca)
+            scaled_plus(dp_e, half_cp, 2.0, dp_e)
+            mul(dp_e, dp_e, s)
+            along = new("along")
+            mul(along, ca, ge)
+            mul(tmp, dp_h, he)
+            add(along, along, tmp)
+            de = new("de")
+            sub(de, along, dp_e)
+            srn = new("srn")
+            mul(srn, s, rn)
+            radial = new("radial")
+            mul(radial, t, t)
+            affine(radial, radial, -1.0, 1.0)
+            mul(radial, radial, ratio_rows[:, rows])
+            with_const(tmp, t, MAXNORM, ALU.is_le)
+            mul(radial, radial, tmp)
+            mul(radial, radial, de)
+            mul(along, along, srn)
+            sub(radial, radial, along)
+            mul(radial, radial, rn)
+            mul(beta[:, rows], radial, fac)
+            with_const(tmp, sum_zz[:, rows], 0.0, ALU.is_gt)
+            mul(srn, srn, tmp)
+            mul(srn, srn, fac)
+            mul(alpha[:, rows], srn, ca)
+            mul(gamma[:, rows], srn, dp_h)
+
+        with tc.tile_pool(name="load", bufs=3) as load, tc.tile_pool(name="work", bufs=2) as work:
+            bias_rows = work.tile([P, D_OUT], BF16)
+            nc.sync.dma_start(out=bias_rows[:], in_=bias.partition_broadcast(P))
+            nc.sync.dma_start(
+                out=ratio_rows[:].rearrange("p (c j) -> p c j", j=PACK),
+                in_=ratio.rearrange("(c p j) o -> p c (j o)", p=P, j=PACK),
+            )
+            bb = small.tile([P, 1], F32, name="bb")[:]
+            junk_b = work.tile([P, D_OUT], F32, tag="junk_v")
+            dot(bb, junk_b[:], bias_rows[:], bias_rows[:])
+            nb = small.tile([P, 1], F32, name="nb")[:]
+            with_const(nb, bb, MIN_NORM, ALU.max)
+            nc.scalar.sqrt(nb, nb)
+            scale_b = small.tile([P, 1], F32, name="scale_b")[:]
+            nc.scalar.activation(out=scale_b, in_=nb, func=FUNC.Tanh)
+            with_const(scale_b, scale_b, MAXNORM, ALU.min)
+            nc.vector.reciprocal(out=nb, in_=nb)
+            mul(scale_b, scale_b, nb)
+            with_const(hb[:], bias_rows[:], scale_b, ALU.mult)
+            mul(y2[:], scale_b, scale_b)
+            mul(y2[:], y2[:], bb)
+            with_const(one_plus_y2[:], y2[:], 1.0, ALU.add)
+
+            for c in range(CHUNKS):
+                z_rows = load.tile([P, PACK, D_OUT], F32)
+                nc.sync.dma_start(out=z_rows[:], in_=z_chunks[c])
+                nc.sync.dma_start(out=g_all[:, c], in_=g_chunks[c])
+                x_rows = load.tile([P, PACK, D_IN], BF16)
+                nc.sync.dma_start(out=x_rows[:], in_=x_chunks[c])
+                for j in range(PACK):
+                    r = c * PACK + j
+                    junk_s = work.tile([P, D_OUT], BF16)
+                    nc.scalar.activation(
+                        out=junk_s[:], in_=z_rows[:, j], func=FUNC.Square, accum_out=sum_zz[:, r : r + 1]
+                    )
+                    junk_v = work.tile([P, D_OUT], F32, tag="junk_v")
+                    dot(sum_zh[:, r : r + 1], junk_v[:], z_rows[:, j], hb[:])
+                    junk_v = work.tile([P, D_OUT], F32, tag="junk_v")
+                    dot(sum_gz[:, r : r + 1], junk_v[:], g_all[:, c, j], z_rows[:, j])
+                    junk_v = work.tile([P, D_OUT], F32, tag="junk_v")
+                    dot(sum_gh[:, r : r + 1], junk_v[:], g_all[:, c, j], hb[:])
+                x_grouped = work.tile([P, D_IN, PACK], BF16, align_bytes=64)
+                nc.scalar.copy(
+                    out=x_grouped[:].rearrange("p (w i) j -> p w j i", i=4),
+                    in_=x_rows[:].rearrange("p j (w i) -> p w j i", i=4),
+                )
+                nc.vector.quantize_mx(
+                    out=x_codes[:, c].bitcast(E4M3X4),
+                    scales=x_scales[:, c],
+                    in_=x_grouped[:].rearrange("p w j -> p (w j)"),
+                )
+                if (c + 1) % (CHUNKS // BATCHES) == 0:
+                    row_scalars(c // (CHUNKS // BATCHES))
+
+        with tc.tile_pool(name="load2", bufs=3, reuse_waits="tile") as load2, tc.tile_pool(
+            name="work2", bufs=2, reuse_waits="tile"
+        ) as work2, tc.psum_pool(name="acc", bufs=1) as acc_pool:
+            for sweep in range(D_OUT // SWEEP):
+                cols = slice(sweep * SWEEP, (sweep + 1) * SWEEP)
+                acc = {}
+                for m in range(SWEEP // M_TILE):
+                    for n in range(D_IN // N_TILE):
+                        acc[(m, n)] = acc_pool.tile([M_TILE, N_TILE], F32, name="acc%d%d" % (m, n))
+                for c in range(CHUNKS):
+                    z_part = load2.tile([P, PACK, SWEEP], F32)
+                    nc.sync.dma_start(out=z_part[:], in_=z_chunks[c, :, :, cols])
+                    part = work2.tile([P, PACK, SWEEP], F32)
+                    dz_rows = work2.tile([P, PACK, SWEEP], BF16)
+                    for j in range(PACK):
+                        r = c * PACK + j
+                        nc.scalar.activation(
+                            out=part[:, j], in_=hb[:, cols], func=FUNC.Copy, scale=gamma[:, r : r + 1]
+                        )
+                        scaled_plus(part[:, j], z_part[:, j], beta[:, r : r + 1], part[:, j])
+                        scaled_plus(dz_rows[:, j], g_all[:, c, j, cols], alpha[:, r : r + 1], part[:, j])
+                    dz_grouped = work2.tile([P, SWEEP, PACK], BF16, align_bytes=64)
+                    nc.scalar.copy(
+                        out=dz_grouped[:].rearrange("p (w i) j -> p w j i", i=4),
+                        in_=dz_rows[:].rearrange("p j (w i) -> p w j i", i=4),
+                    )
+                    dz_codes = work2.tile([P, SWEEP], U32, align_bytes=64)
+                    dz_scales = work2.tile([P, SWEEP], U8, align_bytes=64)
+                    nc.vector.quantize_mx(
+                        out=dz_codes[:].bitcast(E5M2X4),
+                        scales=dz_scales[:],
+                        in_=dz_grouped[:].rearrange("p w j -> p (w j)"),
+                    )
+                    for m in range(SWEEP // M_TILE):
+                        m_cols = slice(m * M_TILE, (m + 1) * M_TILE)
+                        for n in range(D_IN // N_TILE):
+                            n_cols = slice(n * N_TILE, (n + 1) * N_TILE)
+                            nc.tensor.matmul_mx(
+                                out=acc[(m, n)][:],
+                                lhsT=dz_codes[:, m_cols].bitcast(E5M2X4),
+                                lhsT_scale=dz_scales[:, m_cols],
+                                rhs=x_codes[:, c, n_cols].bitcast(E4M3X4),
+                                rhs_scale=x_scales[:, c, n_cols],
+                                start=(c == 0),
+                                stop=(c == CHUNKS - 1),
+                            )
+                for m in range(SWEEP // M_TILE):
+                    out_rows = slice(sweep * SWEEP + m * M_TILE, sweep * SWEEP + (m + 1) * M_TILE)
+                    for n in range(D_IN // N_TILE):
+                        n_cols = slice(n * N_TILE, (n + 1) * N_TILE)
+                        result = work2.tile([M_TILE, N_TILE], F32)
+                        if n == 0:
+                            nc.scalar.copy(out=result[:], in_=acc[(m, n)][:])
+                        else:
+                            nc.vector.tensor_copy(out=result[:], in_=acc[(m, n)][:])
+                        nc.sync.dma_start(out=out[out_rows, n_cols], in_=result[:])

@@ -1,4 +1,5 @@
 import concourse.mybir as mybir
+from concourse.masks import make_identity
 
 F32 = mybir.dt.float32
 BF16 = mybir.dt.bfloat16
@@ -22,6 +23,8 @@ BATCH_ROWS = ROWS // BATCHES
 N_TILE = 512
 M_TILE = 128
 SWEEP = 512
+WORD_BLOCKS = D_OUT // 2 // P
+PIECES = 3
 MAXNORM = 1.0 - 4e-3
 MIN_NORM = 1e-15
 TINY = 1e-30
@@ -59,7 +62,9 @@ def tile_hyplinear_v_kernel(tc, x, weight, bias, z, ratio, grad_out, out):
             out=junk, in0=a, scalar=1.0, in1=b, op0=ALU.mult, op1=ALU.mult, accum_out=acc
         )
 
-    with tc.tile_pool(name="keep", bufs=1) as keep, tc.tile_pool(name="small", bufs=1) as small:
+    with tc.tile_pool(name="keep", bufs=1) as keep, tc.tile_pool(name="small", bufs=1) as small, tc.tile_pool(
+        name="z_ring", bufs=3
+    ) as z_ring:
         g_all = keep.tile([P, CHUNKS, PACK, D_OUT], BF16)
         x_codes = keep.tile([P, CHUNKS, D_IN], U32, align_bytes=64)
         x_scales = keep.tile([P, CHUNKS, D_IN], U8, align_bytes=64)
@@ -72,11 +77,14 @@ def tile_hyplinear_v_kernel(tc, x, weight, bias, z, ratio, grad_out, out):
         alpha = keep.tile([P, ROWS], F32)
         beta = keep.tile([P, ROWS], F32)
         gamma = keep.tile([P, ROWS], F32)
+        identity = keep.tile([P, P], F32)
+        hb_pieces = keep.tile([P, WORD_BLOCKS, 2, PIECES], BF16)
         y2 = keep.tile([P, 1], F32)
         one_plus_y2 = keep.tile([P, 1], F32)
 
-        def row_scalars(batch):
+        def row_scalars(batch, gh_psum):
             rows = slice(batch * BATCH_ROWS, (batch + 1) * BATCH_ROWS)
+            nc.vector.tensor_reduce(out=sum_gh[:, rows], in_=gh_psum[:], axis=mybir.AxisListType.X, op=ALU.add)
 
             def new(name):
                 fresh = small.tile([P, BATCH_ROWS], F32, name=name)
@@ -194,7 +202,10 @@ def tile_hyplinear_v_kernel(tc, x, weight, bias, z, ratio, grad_out, out):
             mul(alpha[:, rows], srn, ca)
             mul(gamma[:, rows], srn, dp_h)
 
-        with tc.tile_pool(name="load", bufs=3) as load, tc.tile_pool(name="work", bufs=2) as work:
+        with tc.tile_pool(name="work", bufs=2) as work, tc.tile_pool(name="flipped", bufs=4) as flipped, tc.psum_pool(
+            name="flip", bufs=4
+        ) as flip, tc.psum_pool(name="sums", bufs=2) as sums:
+            make_identity(nc, identity[:])
             bias_rows = work.tile([P, D_OUT], BF16)
             nc.sync.dma_start(out=bias_rows[:], in_=bias.partition_broadcast(P))
             nc.sync.dma_start(
@@ -216,12 +227,22 @@ def tile_hyplinear_v_kernel(tc, x, weight, bias, z, ratio, grad_out, out):
             mul(y2[:], scale_b, scale_b)
             mul(y2[:], y2[:], bb)
             with_const(one_plus_y2[:], y2[:], 1.0, ALU.add)
+            bias_cols = small.tile([P, WORD_BLOCKS, 2], BF16)
+            nc.sync.dma_start(out=bias_cols[:], in_=bias.rearrange("(b q e) -> q b e", q=P, e=2))
+            rest = small.tile([P, WORD_BLOCKS, 2], F32)
+            with_const(rest[:], bias_cols[:], scale_b, ALU.mult)
+            for i in range(PIECES):
+                nc.vector.tensor_copy(out=hb_pieces[:, :, :, i], in_=rest[:])
+                if i + 1 < PIECES:
+                    sub(rest[:], rest[:], hb_pieces[:, :, :, i])
 
             for c in range(CHUNKS):
-                z_rows = load.tile([P, PACK, D_OUT], F32)
+                if c % (CHUNKS // BATCHES) == 0:
+                    gh_psum = sums.tile([P, BATCH_ROWS, PIECES], F32)
+                z_rows = z_ring.tile([P, PACK, D_OUT], F32, tag="z")
                 nc.sync.dma_start(out=z_rows[:], in_=z_chunks[c])
                 nc.sync.dma_start(out=g_all[:, c], in_=g_chunks[c])
-                x_rows = load.tile([P, PACK, D_IN], BF16)
+                x_rows = work.tile([P, PACK, D_IN], BF16)
                 nc.sync.dma_start(out=x_rows[:], in_=x_chunks[c])
                 for j in range(PACK):
                     r = c * PACK + j
@@ -233,8 +254,24 @@ def tile_hyplinear_v_kernel(tc, x, weight, bias, z, ratio, grad_out, out):
                     dot(sum_zh[:, r : r + 1], junk_v[:], z_rows[:, j], hb[:])
                     junk_v = work.tile([P, D_OUT], F32, tag="junk_v")
                     dot(sum_gz[:, r : r + 1], junk_v[:], g_all[:, c, j], z_rows[:, j])
-                    junk_v = work.tile([P, D_OUT], F32, tag="junk_v")
-                    dot(sum_gh[:, r : r + 1], junk_v[:], g_all[:, c, j], hb[:])
+                    g_words = g_all[:, c, j].bitcast(F32)
+                    gt_psum = flip.tile([P, WORD_BLOCKS, P], F32)
+                    for b in range(WORD_BLOCKS):
+                        nc.tensor.transpose(gt_psum[:, b, :], g_words[:, b * P : (b + 1) * P], identity[:])
+                    gt = flipped.tile([P, WORD_BLOCKS, P, 2], BF16)
+                    nc.scalar.copy(
+                        out=gt[:].rearrange("q b p e -> q (b p e)"),
+                        in_=gt_psum[:].rearrange("q b p -> q (b p)").bitcast(BF16),
+                    )
+                    for b in range(WORD_BLOCKS):
+                        for e in range(2):
+                            nc.tensor.matmul(
+                                out=gh_psum[:, r % BATCH_ROWS, :],
+                                lhsT=gt[:, b, :, e],
+                                rhs=hb_pieces[:, b, e, :],
+                                start=(b == 0 and e == 0),
+                                stop=(b == WORD_BLOCKS - 1 and e == 1),
+                            )
                 x_grouped = work.tile([P, D_IN, PACK], BF16, align_bytes=64)
                 nc.scalar.copy(
                     out=x_grouped[:].rearrange("p (w i) j -> p w j i", i=4),
@@ -246,11 +283,11 @@ def tile_hyplinear_v_kernel(tc, x, weight, bias, z, ratio, grad_out, out):
                     in_=x_grouped[:].rearrange("p w j -> p (w j)"),
                 )
                 if (c + 1) % (CHUNKS // BATCHES) == 0:
-                    row_scalars(c // (CHUNKS // BATCHES))
+                    row_scalars(c // (CHUNKS // BATCHES), gh_psum)
 
-        with tc.tile_pool(name="load2", bufs=3, reuse_waits="tile") as load2, tc.tile_pool(
-            name="work2", bufs=2, reuse_waits="tile"
-        ) as work2, tc.psum_pool(name="acc", bufs=1) as acc_pool:
+        with tc.tile_pool(name="work2", bufs=3, reuse_waits="tile") as work2, tc.psum_pool(
+            name="acc", bufs=1
+        ) as acc_pool:
             for sweep in range(D_OUT // SWEEP):
                 cols = slice(sweep * SWEEP, (sweep + 1) * SWEEP)
                 acc = {}
@@ -258,7 +295,7 @@ def tile_hyplinear_v_kernel(tc, x, weight, bias, z, ratio, grad_out, out):
                     for n in range(D_IN // N_TILE):
                         acc[(m, n)] = acc_pool.tile([M_TILE, N_TILE], F32, name="acc%d%d" % (m, n))
                 for c in range(CHUNKS):
-                    z_part = load2.tile([P, PACK, SWEEP], F32)
+                    z_part = z_ring.tile([P, PACK, SWEEP], F32, tag="z")
                     nc.sync.dma_start(out=z_part[:], in_=z_chunks[c, :, :, cols])
                     part = work2.tile([P, PACK, SWEEP], F32)
                     dz_rows = work2.tile([P, PACK, SWEEP], BF16)

@@ -18,8 +18,6 @@ D_IN = 1024
 D_OUT = 1024
 CHUNKS = TOKENS // K_PASS
 ROWS = CHUNKS * PACK
-BATCHES = 2
-BATCH_ROWS = ROWS // BATCHES
 N_TILE = 512
 M_TILE = 128
 SWEEP = 512
@@ -62,163 +60,163 @@ def tile_hyplinear_v_kernel(tc, x, weight, bias, z, ratio, grad_out, out):
             out=junk, in0=a, scalar=1.0, in1=b, op0=ALU.mult, op1=ALU.mult, accum_out=acc
         )
 
-    with tc.tile_pool(name="keep", bufs=1) as keep, tc.tile_pool(name="small", bufs=1) as small, tc.tile_pool(
-        name="z_ring", bufs=3
-    ) as z_ring:
+    with tc.tile_pool(name="keep", bufs=1) as keep, tc.tile_pool(name="z_ring", bufs=3) as z_ring:
         g_all = keep.tile([P, CHUNKS, PACK, D_OUT], BF16)
         x_codes = keep.tile([P, CHUNKS, D_IN], U32, align_bytes=64)
         x_scales = keep.tile([P, CHUNKS, D_IN], U8, align_bytes=64)
         hb = keep.tile([P, D_OUT], F32)
-        ratio_rows = keep.tile([P, ROWS], F32)
-        sum_zz = keep.tile([P, ROWS], F32)
-        sum_zh = keep.tile([P, ROWS], F32)
-        sum_gz = keep.tile([P, ROWS], F32)
-        sum_gh = keep.tile([P, ROWS], F32)
-        alpha = keep.tile([P, ROWS], F32)
-        beta = keep.tile([P, ROWS], F32)
-        gamma = keep.tile([P, ROWS], F32)
         identity = keep.tile([P, P], F32)
         hb_pieces = keep.tile([P, WORD_BLOCKS, 2, PIECES], BF16)
         y2 = keep.tile([P, 1], F32)
         one_plus_y2 = keep.tile([P, 1], F32)
 
-        def row_scalars(batch, gh_psum):
-            rows = slice(batch * BATCH_ROWS, (batch + 1) * BATCH_ROWS)
-            nc.vector.tensor_reduce(out=sum_gh[:, rows], in_=gh_psum[:], axis=mybir.AxisListType.X, op=ALU.add)
+        def per_row(name):
+            fresh = keep.tile([P, ROWS], F32, name=name)
+            return fresh[:]
 
-            def new(name):
-                fresh = small.tile([P, BATCH_ROWS], F32, name=name)
-                return fresh[:]
+        ratio_rows = per_row("ratio_rows")
+        sum_zz = per_row("sum_zz")
+        sum_zh = per_row("sum_zh")
+        sum_gz = per_row("sum_gz")
+        alpha = per_row("alpha")
+        beta = per_row("beta")
+        gamma = per_row("gamma")
+        rn = per_row("rn")
+        s = per_row("s")
+        he = per_row("he")
+        ca = per_row("ca")
+        cb = per_row("cb")
+        cas = per_row("cas")
+        ve = per_row("ve")
+        vh = per_row("vh")
+        w_mu = per_row("w_mu")
+        w_qv = per_row("w_qv")
+        srn = per_row("srn")
+        radial = per_row("radial")
+        rnfac = per_row("rnfac")
+        sfac = per_row("sfac")
 
-            n = new("n")
-            with_const(n, sum_zz[:, rows], MIN_NORM, ALU.max)
+        def scalars_from_z():
+            n = per_row("n")
+            with_const(n, sum_zz, MIN_NORM, ALU.max)
             nc.scalar.sqrt(n, n)
-            rn = new("rn")
             nc.vector.reciprocal(out=rn, in_=n)
-            t = new("t")
-            mul(t, n, ratio_rows[:, rows])
+            t = per_row("t")
+            mul(t, n, ratio_rows)
             nc.scalar.activation(out=t, in_=t, func=FUNC.Tanh)
-            s = new("s")
+            mul(he, sum_zh, rn)
             with_const(s, t, MAXNORM, ALU.min)
-            he = new("he")
-            mul(he, sum_zh[:, rows], rn)
-            xy = new("xy")
+            xy = per_row("xy")
             mul(xy, s, he)
-            x2 = new("x2")
+            x2 = per_row("x2")
             mul(x2, s, s)
-            ca = new("ca")
             affine(ca, xy, 2.0, one_plus_y2[:, 0:1])
-            cb = new("cb")
             affine(cb, x2, -1.0, 1.0)
-            den = new("den")
+            den = per_row("den")
             affine(den, x2, y2[:, 0:1], 1.0)
             scaled_plus(den, xy, 2.0, den)
             with_const(den, den, MIN_NORM, ALU.max)
-            rden = new("rden")
+            rden = per_row("rden")
             nc.vector.reciprocal(out=rden, in_=den)
-            cas = new("cas")
-            mul(cas, ca, s)
-            ve = new("ve")
-            mul(ve, cb, he)
-            add(ve, ve, cas)
-            vh = new("vh")
-            mul(vh, cas, he)
-            scaled_plus(vh, cb, y2[:, 0:1], vh)
-            vv = new("vv")
-            tmp = new("tmp")
-            mul(vv, cas, ve)
-            mul(tmp, cb, vh)
-            add(vv, vv, tmp)
-            nv = new("nv")
-            mul(nv, rden, rden)
-            mul(nv, nv, vv)
-            with_const(nv, nv, MIN_NORM, ALU.max)
-            nc.scalar.sqrt(nv, nv)
-            v_out = new("v_out")
-            with_const(v_out, nv, MAXNORM, ALU.is_gt)
-            fac = new("fac")
-            with_const(fac, nv, MAXNORM, ALU.max)
+            amb = per_row("amb")
+            sub(amb, ca, cb)
+            vv = per_row("vv")
+            mul(vv, amb, rden)
+            v_out = per_row("v_out")
+            with_const(v_out, vv, MAXNORM * MAXNORM, ALU.is_gt)
+            fac = per_row("fac")
+            with_const(fac, vv, MAXNORM * MAXNORM, ALU.max)
+            nc.scalar.sqrt(fac, fac)
             nc.vector.reciprocal(out=fac, in_=fac)
             scaled_plus(fac, rden, MAXNORM, fac, op1=ALU.mult)
-            rvv = new("rvv")
-            with_const(rvv, vv, TINY, ALU.max)
-            nc.vector.reciprocal(out=rvv, in_=rvv)
-            mul(rvv, rvv, v_out)
-            ge = new("ge")
-            mul(ge, sum_gz[:, rows], rn)
-            gh = sum_gh[:, rows]
-            mu = new("mu")
-            mul(mu, cas, ge)
+            mul(cas, ca, s)
+            mul(ve, cb, he)
+            add(ve, ve, cas)
+            mul(vh, cas, he)
+            scaled_plus(vh, cb, y2[:, 0:1], vh)
+            with_const(w_mu, amb, TINY, ALU.max)
+            nc.vector.reciprocal(out=w_mu, in_=w_mu)
+            mul(w_mu, w_mu, rden)
+            mul(w_mu, w_mu, v_out)
+            affine(w_qv, v_out, -1.0, 1.0)
+            mul(w_qv, w_qv, rden)
+            mul(srn, s, rn)
+            mul(radial, t, t)
+            affine(radial, radial, -1.0, 1.0)
+            mul(radial, radial, ratio_rows)
+            with_const(t, t, MAXNORM, ALU.is_le)
+            mul(radial, radial, t)
+            mul(rnfac, rn, fac)
+            with_const(sfac, sum_zz, 0.0, ALU.is_gt)
+            mul(sfac, sfac, srn)
+            mul(sfac, sfac, fac)
+            mul(alpha, sfac, ca)
+
+        def scalars_from_g(gh_psum):
+            gh = per_row("gh")
+            nc.vector.tensor_reduce(out=gh, in_=gh_psum[:], axis=mybir.AxisListType.X, op=ALU.add)
+            ge = per_row("ge")
+            mul(ge, sum_gz, rn)
+            tmp = per_row("tmp")
+            gv = per_row("gv")
+            mul(gv, cas, ge)
             mul(tmp, cb, gh)
-            add(mu, mu, tmp)
-            mul(mu, mu, rvv)
-            qe = new("qe")
+            add(gv, gv, tmp)
+            mu = per_row("mu")
+            mul(mu, gv, w_mu)
+            qv = per_row("qv")
+            mul(qv, gv, w_qv)
+            qe = per_row("qe")
             mul(qe, mu, ve)
             sub(qe, ge, qe)
-            qh = new("qh")
+            qh = per_row("qh")
             mul(qh, mu, vh)
             sub(qh, gh, qh)
-            qv = new("qv")
-            mul(qv, cas, qe)
-            mul(tmp, cb, qh)
-            add(qv, qv, tmp)
-            mul(qv, qv, rden)
-            half_ch = new("half_ch")
+            half_ch = per_row("half_ch")
             mul(half_ch, s, qe)
             sub(half_ch, half_ch, qv)
-            half_cp = new("half_cp")
+            half_cp = per_row("half_cp")
             scaled_plus(half_cp, qv, y2[:, 0:1], qh)
-            mua = new("mua")
+            mua = per_row("mua")
             mul(mua, mu, ca)
-            dp_h = new("dp_h")
+            dp_h = per_row("dp_h")
             mul(dp_h, mua, cb)
             scaled_plus(dp_h, half_ch, 2.0, dp_h, op1=ALU.subtract)
-            dp_e = new("dp_e")
+            dp_e = per_row("dp_e")
             mul(dp_e, mua, ca)
             scaled_plus(dp_e, half_cp, 2.0, dp_e)
             mul(dp_e, dp_e, s)
-            along = new("along")
+            along = per_row("along")
             mul(along, ca, ge)
             mul(tmp, dp_h, he)
             add(along, along, tmp)
-            de = new("de")
+            de = per_row("de")
             sub(de, along, dp_e)
-            srn = new("srn")
-            mul(srn, s, rn)
-            radial = new("radial")
-            mul(radial, t, t)
-            affine(radial, radial, -1.0, 1.0)
-            mul(radial, radial, ratio_rows[:, rows])
-            with_const(tmp, t, MAXNORM, ALU.is_le)
-            mul(radial, radial, tmp)
-            mul(radial, radial, de)
+            mul(de, de, radial)
             mul(along, along, srn)
-            sub(radial, radial, along)
-            mul(radial, radial, rn)
-            mul(beta[:, rows], radial, fac)
-            with_const(tmp, sum_zz[:, rows], 0.0, ALU.is_gt)
-            mul(srn, srn, tmp)
-            mul(srn, srn, fac)
-            mul(alpha[:, rows], srn, ca)
-            mul(gamma[:, rows], srn, dp_h)
+            sub(de, de, along)
+            mul(beta, de, rnfac)
+            mul(gamma, sfac, dp_h)
 
         with tc.tile_pool(name="work", bufs=2) as work, tc.tile_pool(name="flipped", bufs=4) as flipped, tc.psum_pool(
             name="flip", bufs=4
-        ) as flip, tc.psum_pool(name="sums", bufs=2) as sums:
-            make_identity(nc, identity[:])
+        ) as flip, tc.psum_pool(name="sums", bufs=1) as sums:
             bias_rows = work.tile([P, D_OUT], BF16)
             nc.sync.dma_start(out=bias_rows[:], in_=bias.partition_broadcast(P))
-            nc.sync.dma_start(
-                out=ratio_rows[:].rearrange("p (c j) -> p c j", j=PACK),
+            bias_cols = keep.tile([P, WORD_BLOCKS, 2], BF16)
+            nc.scalar.dma_start(out=bias_cols[:], in_=bias.rearrange("(b q e) -> q b e", q=P, e=2))
+            nc.scalar.dma_start(
+                out=ratio_rows.rearrange("p (c j) -> p c j", j=PACK),
                 in_=ratio.rearrange("(c p j) o -> p c (j o)", p=P, j=PACK),
             )
-            bb = small.tile([P, 1], F32, name="bb")[:]
+            make_identity(nc, identity[:])
+            bb = keep.tile([P, 1], F32, name="bb")[:]
             junk_b = work.tile([P, D_OUT], F32, tag="junk_v")
             dot(bb, junk_b[:], bias_rows[:], bias_rows[:])
-            nb = small.tile([P, 1], F32, name="nb")[:]
+            nb = keep.tile([P, 1], F32, name="nb")[:]
             with_const(nb, bb, MIN_NORM, ALU.max)
             nc.scalar.sqrt(nb, nb)
-            scale_b = small.tile([P, 1], F32, name="scale_b")[:]
+            scale_b = keep.tile([P, 1], F32, name="scale_b")[:]
             nc.scalar.activation(out=scale_b, in_=nb, func=FUNC.Tanh)
             with_const(scale_b, scale_b, MAXNORM, ALU.min)
             nc.vector.reciprocal(out=nb, in_=nb)
@@ -227,21 +225,27 @@ def tile_hyplinear_v_kernel(tc, x, weight, bias, z, ratio, grad_out, out):
             mul(y2[:], scale_b, scale_b)
             mul(y2[:], y2[:], bb)
             with_const(one_plus_y2[:], y2[:], 1.0, ALU.add)
-            bias_cols = small.tile([P, WORD_BLOCKS, 2], BF16)
-            nc.sync.dma_start(out=bias_cols[:], in_=bias.rearrange("(b q e) -> q b e", q=P, e=2))
-            rest = small.tile([P, WORD_BLOCKS, 2], F32)
+            rest = keep.tile([P, WORD_BLOCKS, 2], F32)
             with_const(rest[:], bias_cols[:], scale_b, ALU.mult)
             for i in range(PIECES):
                 nc.vector.tensor_copy(out=hb_pieces[:, :, :, i], in_=rest[:])
                 if i + 1 < PIECES:
                     sub(rest[:], rest[:], hb_pieces[:, :, :, i])
 
+            gh_psum = sums.tile([P, ROWS, PIECES], F32)
+
+            def sums_with_g(c, z_rows):
+                for j in range(PACK):
+                    r = c * PACK + j
+                    junk_v = work.tile([P, D_OUT], F32, tag="junk_v")
+                    dot(sum_gz[:, r : r + 1], junk_v[:], g_all[:, c, j], z_rows[:, j])
+
+            z_before = None
             for c in range(CHUNKS):
-                if c % (CHUNKS // BATCHES) == 0:
-                    gh_psum = sums.tile([P, BATCH_ROWS, PIECES], F32)
                 z_rows = z_ring.tile([P, PACK, D_OUT], F32, tag="z")
-                nc.sync.dma_start(out=z_rows[:], in_=z_chunks[c])
-                nc.sync.dma_start(out=g_all[:, c], in_=g_chunks[c])
+                for j in range(PACK):
+                    nc.sync.dma_start(out=z_rows[:, j], in_=z_chunks[c, :, j])
+                    nc.sync.dma_start(out=g_all[:, c, j], in_=g_chunks[c, :, j])
                 x_rows = work.tile([P, PACK, D_IN], BF16)
                 nc.sync.dma_start(out=x_rows[:], in_=x_chunks[c])
                 for j in range(PACK):
@@ -252,8 +256,6 @@ def tile_hyplinear_v_kernel(tc, x, weight, bias, z, ratio, grad_out, out):
                     )
                     junk_v = work.tile([P, D_OUT], F32, tag="junk_v")
                     dot(sum_zh[:, r : r + 1], junk_v[:], z_rows[:, j], hb[:])
-                    junk_v = work.tile([P, D_OUT], F32, tag="junk_v")
-                    dot(sum_gz[:, r : r + 1], junk_v[:], g_all[:, c, j], z_rows[:, j])
                     g_words = g_all[:, c, j].bitcast(F32)
                     gt_psum = flip.tile([P, WORD_BLOCKS, P], F32)
                     for b in range(WORD_BLOCKS):
@@ -266,7 +268,7 @@ def tile_hyplinear_v_kernel(tc, x, weight, bias, z, ratio, grad_out, out):
                     for b in range(WORD_BLOCKS):
                         for e in range(2):
                             nc.tensor.matmul(
-                                out=gh_psum[:, r % BATCH_ROWS, :],
+                                out=gh_psum[:, r, :],
                                 lhsT=gt[:, b, :, e],
                                 rhs=hb_pieces[:, b, e, :],
                                 start=(b == 0 and e == 0),
@@ -282,8 +284,12 @@ def tile_hyplinear_v_kernel(tc, x, weight, bias, z, ratio, grad_out, out):
                     scales=x_scales[:, c],
                     in_=x_grouped[:].rearrange("p w j -> p (w j)"),
                 )
-                if (c + 1) % (CHUNKS // BATCHES) == 0:
-                    row_scalars(c // (CHUNKS // BATCHES), gh_psum)
+                if c > 0:
+                    sums_with_g(c - 1, z_before)
+                z_before = z_rows
+            scalars_from_z()
+            sums_with_g(CHUNKS - 1, z_before)
+            scalars_from_g(gh_psum)
 
         with tc.tile_pool(name="work2", bufs=3, reuse_waits="tile") as work2, tc.psum_pool(
             name="acc", bufs=1

import concourse.mybir as mybir
from concourse.masks import make_identity

F32 = mybir.dt.float32
BF16 = mybir.dt.bfloat16
U32 = mybir.dt.uint32
U8 = mybir.dt.uint8
E4M3X4 = mybir.dt.float8_e4m3fn_x4
E5M2X4 = mybir.dt.float8_e5m2_x4
ALU = mybir.AluOpType
FUNC = mybir.ActivationFunctionType

P = 128
PACK = 4
K_PASS = P * PACK
TOKENS = 4096
D_IN = 1024
D_OUT = 1024
CHUNKS = TOKENS // K_PASS
ROWS = CHUNKS * PACK
N_TILE = 512
M_TILE = 128
SWEEP = 512
WORD_BLOCKS = D_OUT // 2 // P
PIECES = 3
MAXNORM = 1.0 - 4e-3
MIN_NORM = 1e-15
TINY = 1e-30

FLOPS = 2 * TOKENS * D_IN * D_OUT
BYTES = TOKENS * D_IN * 2 + TOKENS * D_OUT * (4 + 2) + TOKENS * 4 + D_OUT * 2 + D_OUT * D_IN * 4


def tile_hyplinear_v_kernel(tc, x, weight, bias, z, ratio, grad_out, out):
    nc = tc.nc
    x_chunks = x.rearrange("(c p j) w -> c p j w", p=P, j=PACK)
    z_chunks = z.rearrange("(c p j) w -> c p j w", p=P, j=PACK)
    g_chunks = grad_out.rearrange("(c p j) w -> c p j w", p=P, j=PACK)

    def mul(o, a, b):
        nc.vector.tensor_tensor(out=o, in0=a, in1=b, op=ALU.mult)

    def add(o, a, b):
        nc.vector.tensor_tensor(out=o, in0=a, in1=b, op=ALU.add)

    def sub(o, a, b):
        nc.vector.tensor_tensor(out=o, in0=a, in1=b, op=ALU.subtract)

    def affine(o, a, m, b):
        nc.vector.tensor_scalar(out=o, in0=a, scalar1=m, scalar2=b, op0=ALU.mult, op1=ALU.add)

    def with_const(o, a, c, op):
        nc.vector.tensor_scalar(out=o, in0=a, scalar1=c, scalar2=None, op0=op)

    def scaled_plus(o, a, m, b, op1=ALU.add):
        nc.vector.scalar_tensor_tensor(out=o, in0=a, scalar=m, in1=b, op0=ALU.mult, op1=op1)

    def dot(acc, junk, a, b):
        nc.vector.scalar_tensor_tensor(
            out=junk, in0=a, scalar=1.0, in1=b, op0=ALU.mult, op1=ALU.mult, accum_out=acc
        )

    with tc.tile_pool(name="keep", bufs=1) as keep, tc.tile_pool(name="z_ring", bufs=3) as z_ring:
        g_all = keep.tile([P, CHUNKS, PACK, D_OUT], BF16)
        x_codes = keep.tile([P, CHUNKS, D_IN], U32, align_bytes=64)
        x_scales = keep.tile([P, CHUNKS, D_IN], U8, align_bytes=64)
        hb = keep.tile([P, D_OUT], F32)
        identity = keep.tile([P, P], F32)
        hb_pieces = keep.tile([P, WORD_BLOCKS, 2, PIECES], BF16)
        y2 = keep.tile([P, 1], F32)
        one_plus_y2 = keep.tile([P, 1], F32)

        def per_row(name):
            fresh = keep.tile([P, ROWS], F32, name=name)
            return fresh[:]

        ratio_rows = per_row("ratio_rows")
        sum_zz = per_row("sum_zz")
        sum_zh = per_row("sum_zh")
        sum_gz = per_row("sum_gz")
        alpha = per_row("alpha")
        beta = per_row("beta")
        gamma = per_row("gamma")
        rn = per_row("rn")
        s = per_row("s")
        he = per_row("he")
        ca = per_row("ca")
        cb = per_row("cb")
        cas = per_row("cas")
        ve = per_row("ve")
        vh = per_row("vh")
        w_mu = per_row("w_mu")
        w_qv = per_row("w_qv")
        srn = per_row("srn")
        radial = per_row("radial")
        rnfac = per_row("rnfac")
        sfac = per_row("sfac")

        def scalars_from_z():
            n = per_row("n")
            with_const(n, sum_zz, MIN_NORM, ALU.max)
            nc.scalar.sqrt(n, n)
            nc.vector.reciprocal(out=rn, in_=n)
            t = per_row("t")
            mul(t, n, ratio_rows)
            nc.scalar.activation(out=t, in_=t, func=FUNC.Tanh)
            mul(he, sum_zh, rn)
            with_const(s, t, MAXNORM, ALU.min)
            xy = per_row("xy")
            mul(xy, s, he)
            x2 = per_row("x2")
            mul(x2, s, s)
            affine(ca, xy, 2.0, one_plus_y2[:, 0:1])
            affine(cb, x2, -1.0, 1.0)
            den = per_row("den")
            affine(den, x2, y2[:, 0:1], 1.0)
            scaled_plus(den, xy, 2.0, den)
            with_const(den, den, MIN_NORM, ALU.max)
            rden = per_row("rden")
            nc.vector.reciprocal(out=rden, in_=den)
            amb = per_row("amb")
            sub(amb, ca, cb)
            vv = per_row("vv")
            mul(vv, amb, rden)
            v_out = per_row("v_out")
            with_const(v_out, vv, MAXNORM * MAXNORM, ALU.is_gt)
            fac = per_row("fac")
            with_const(fac, vv, MAXNORM * MAXNORM, ALU.max)
            nc.scalar.sqrt(fac, fac)
            nc.vector.reciprocal(out=fac, in_=fac)
            scaled_plus(fac, rden, MAXNORM, fac, op1=ALU.mult)
            mul(cas, ca, s)
            mul(ve, cb, he)
            add(ve, ve, cas)
            mul(vh, cas, he)
            scaled_plus(vh, cb, y2[:, 0:1], vh)
            with_const(w_mu, amb, TINY, ALU.max)
            nc.vector.reciprocal(out=w_mu, in_=w_mu)
            mul(w_mu, w_mu, rden)
            mul(w_mu, w_mu, v_out)
            affine(w_qv, v_out, -1.0, 1.0)
            mul(w_qv, w_qv, rden)
            mul(srn, s, rn)
            mul(radial, t, t)
            affine(radial, radial, -1.0, 1.0)
            mul(radial, radial, ratio_rows)
            with_const(t, t, MAXNORM, ALU.is_le)
            mul(radial, radial, t)
            mul(rnfac, rn, fac)
            with_const(sfac, sum_zz, 0.0, ALU.is_gt)
            mul(sfac, sfac, srn)
            mul(sfac, sfac, fac)
            mul(alpha, sfac, ca)

        def scalars_from_g(gh_psum):
            gh = per_row("gh")
            nc.vector.tensor_reduce(out=gh, in_=gh_psum[:], axis=mybir.AxisListType.X, op=ALU.add)
            ge = per_row("ge")
            mul(ge, sum_gz, rn)
            tmp = per_row("tmp")
            gv = per_row("gv")
            mul(gv, cas, ge)
            mul(tmp, cb, gh)
            add(gv, gv, tmp)
            mu = per_row("mu")
            mul(mu, gv, w_mu)
            qv = per_row("qv")
            mul(qv, gv, w_qv)
            qe = per_row("qe")
            mul(qe, mu, ve)
            sub(qe, ge, qe)
            qh = per_row("qh")
            mul(qh, mu, vh)
            sub(qh, gh, qh)
            half_ch = per_row("half_ch")
            mul(half_ch, s, qe)
            sub(half_ch, half_ch, qv)
            half_cp = per_row("half_cp")
            scaled_plus(half_cp, qv, y2[:, 0:1], qh)
            mua = per_row("mua")
            mul(mua, mu, ca)
            dp_h = per_row("dp_h")
            mul(dp_h, mua, cb)
            scaled_plus(dp_h, half_ch, 2.0, dp_h, op1=ALU.subtract)
            dp_e = per_row("dp_e")
            mul(dp_e, mua, ca)
            scaled_plus(dp_e, half_cp, 2.0, dp_e)
            mul(dp_e, dp_e, s)
            along = per_row("along")
            mul(along, ca, ge)
            mul(tmp, dp_h, he)
            add(along, along, tmp)
            de = per_row("de")
            sub(de, along, dp_e)
            mul(de, de, radial)
            mul(along, along, srn)
            sub(de, de, along)
            mul(beta, de, rnfac)
            mul(gamma, sfac, dp_h)

        with tc.tile_pool(name="work", bufs=2) as work, tc.tile_pool(name="flipped", bufs=4) as flipped, tc.psum_pool(
            name="flip", bufs=4
        ) as flip, tc.psum_pool(name="sums", bufs=1) as sums:
            bias_rows = work.tile([P, D_OUT], BF16)
            nc.sync.dma_start(out=bias_rows[:], in_=bias.partition_broadcast(P))
            bias_cols = keep.tile([P, WORD_BLOCKS, 2], BF16)
            nc.scalar.dma_start(out=bias_cols[:], in_=bias.rearrange("(b q e) -> q b e", q=P, e=2))
            nc.scalar.dma_start(
                out=ratio_rows.rearrange("p (c j) -> p c j", j=PACK),
                in_=ratio.rearrange("(c p j) o -> p c (j o)", p=P, j=PACK),
            )
            make_identity(nc, identity[:])
            bb = keep.tile([P, 1], F32, name="bb")[:]
            junk_b = work.tile([P, D_OUT], F32, tag="junk_v")
            dot(bb, junk_b[:], bias_rows[:], bias_rows[:])
            nb = keep.tile([P, 1], F32, name="nb")[:]
            with_const(nb, bb, MIN_NORM, ALU.max)
            nc.scalar.sqrt(nb, nb)
            scale_b = keep.tile([P, 1], F32, name="scale_b")[:]
            nc.scalar.activation(out=scale_b, in_=nb, func=FUNC.Tanh)
            with_const(scale_b, scale_b, MAXNORM, ALU.min)
            nc.vector.reciprocal(out=nb, in_=nb)
            mul(scale_b, scale_b, nb)
            with_const(hb[:], bias_rows[:], scale_b, ALU.mult)
            mul(y2[:], scale_b, scale_b)
            mul(y2[:], y2[:], bb)
            with_const(one_plus_y2[:], y2[:], 1.0, ALU.add)
            rest = keep.tile([P, WORD_BLOCKS, 2], F32)
            with_const(rest[:], bias_cols[:], scale_b, ALU.mult)
            for i in range(PIECES):
                nc.vector.tensor_copy(out=hb_pieces[:, :, :, i], in_=rest[:])
                if i + 1 < PIECES:
                    sub(rest[:], rest[:], hb_pieces[:, :, :, i])

            gh_psum = sums.tile([P, ROWS, PIECES], F32)

            def sums_with_g(c, z_rows):
                for j in range(PACK):
                    r = c * PACK + j
                    junk_v = work.tile([P, D_OUT], F32, tag="junk_v")
                    dot(sum_gz[:, r : r + 1], junk_v[:], g_all[:, c, j], z_rows[:, j])

            z_before = None
            for c in range(CHUNKS):
                z_rows = z_ring.tile([P, PACK, D_OUT], F32, tag="z")
                for j in range(PACK):
                    nc.sync.dma_start(out=z_rows[:, j], in_=z_chunks[c, :, j])
                    nc.sync.dma_start(out=g_all[:, c, j], in_=g_chunks[c, :, j])
                x_rows = work.tile([P, PACK, D_IN], BF16)
                nc.sync.dma_start(out=x_rows[:], in_=x_chunks[c])
                for j in range(PACK):
                    r = c * PACK + j
                    junk_s = work.tile([P, D_OUT], BF16)
                    nc.scalar.activation(
                        out=junk_s[:], in_=z_rows[:, j], func=FUNC.Square, accum_out=sum_zz[:, r : r + 1]
                    )
                    junk_v = work.tile([P, D_OUT], F32, tag="junk_v")
                    dot(sum_zh[:, r : r + 1], junk_v[:], z_rows[:, j], hb[:])
                    g_words = g_all[:, c, j].bitcast(F32)
                    gt_psum = flip.tile([P, WORD_BLOCKS, P], F32)
                    for b in range(WORD_BLOCKS):
                        nc.tensor.transpose(gt_psum[:, b, :], g_words[:, b * P : (b + 1) * P], identity[:])
                    gt = flipped.tile([P, WORD_BLOCKS, P, 2], BF16)
                    nc.scalar.copy(
                        out=gt[:].rearrange("q b p e -> q (b p e)"),
                        in_=gt_psum[:].rearrange("q b p -> q (b p)").bitcast(BF16),
                    )
                    for b in range(WORD_BLOCKS):
                        for e in range(2):
                            nc.tensor.matmul(
                                out=gh_psum[:, r, :],
                                lhsT=gt[:, b, :, e],
                                rhs=hb_pieces[:, b, e, :],
                                start=(b == 0 and e == 0),
                                stop=(b == WORD_BLOCKS - 1 and e == 1),
                            )
                x_grouped = work.tile([P, D_IN, PACK], BF16, align_bytes=64)
                nc.scalar.copy(
                    out=x_grouped[:].rearrange("p (w i) j -> p w j i", i=4),
                    in_=x_rows[:].rearrange("p j (w i) -> p w j i", i=4),
                )
                nc.vector.quantize_mx(
                    out=x_codes[:, c].bitcast(E4M3X4),
                    scales=x_scales[:, c],
                    in_=x_grouped[:].rearrange("p w j -> p (w j)"),
                )
                if c > 0:
                    sums_with_g(c - 1, z_before)
                z_before = z_rows
            scalars_from_z()
            sums_with_g(CHUNKS - 1, z_before)
            scalars_from_g(gh_psum)

        with tc.tile_pool(name="work2", bufs=3, reuse_waits="tile") as work2, tc.psum_pool(
            name="acc", bufs=1
        ) as acc_pool:
            for sweep in range(D_OUT // SWEEP):
                cols = slice(sweep * SWEEP, (sweep + 1) * SWEEP)
                acc = {}
                for m in range(SWEEP // M_TILE):
                    for n in range(D_IN // N_TILE):
                        acc[(m, n)] = acc_pool.tile([M_TILE, N_TILE], F32, name="acc%d%d" % (m, n))
                for c in range(CHUNKS):
                    z_part = z_ring.tile([P, PACK, SWEEP], F32, tag="z")
                    nc.sync.dma_start(out=z_part[:], in_=z_chunks[c, :, :, cols])
                    part = work2.tile([P, PACK, SWEEP], F32)
                    dz_rows = work2.tile([P, PACK, SWEEP], BF16)
                    for j in range(PACK):
                        r = c * PACK + j
                        nc.scalar.activation(
                            out=part[:, j], in_=hb[:, cols], func=FUNC.Copy, scale=gamma[:, r : r + 1]
                        )
                        scaled_plus(part[:, j], z_part[:, j], beta[:, r : r + 1], part[:, j])
                        scaled_plus(dz_rows[:, j], g_all[:, c, j, cols], alpha[:, r : r + 1], part[:, j])
                    dz_grouped = work2.tile([P, SWEEP, PACK], BF16, align_bytes=64)
                    nc.scalar.copy(
                        out=dz_grouped[:].rearrange("p (w i) j -> p w j i", i=4),
                        in_=dz_rows[:].rearrange("p j (w i) -> p w j i", i=4),
                    )
                    dz_codes = work2.tile([P, SWEEP], U32, align_bytes=64)
                    dz_scales = work2.tile([P, SWEEP], U8, align_bytes=64)
                    nc.vector.quantize_mx(
                        out=dz_codes[:].bitcast(E5M2X4),
                        scales=dz_scales[:],
                        in_=dz_grouped[:].rearrange("p w j -> p (w j)"),
                    )
                    for m in range(SWEEP // M_TILE):
                        m_cols = slice(m * M_TILE, (m + 1) * M_TILE)
                        for n in range(D_IN // N_TILE):
                            n_cols = slice(n * N_TILE, (n + 1) * N_TILE)
                            nc.tensor.matmul_mx(
                                out=acc[(m, n)][:],
                                lhsT=dz_codes[:, m_cols].bitcast(E5M2X4),
                                lhsT_scale=dz_scales[:, m_cols],
                                rhs=x_codes[:, c, n_cols].bitcast(E4M3X4),
                                rhs_scale=x_scales[:, c, n_cols],
                                start=(c == 0),
                                stop=(c == CHUNKS - 1),
                            )
                for m in range(SWEEP // M_TILE):
                    out_rows = slice(sweep * SWEEP + m * M_TILE, sweep * SWEEP + (m + 1) * M_TILE)
                    for n in range(D_IN // N_TILE):
                        n_cols = slice(n * N_TILE, (n + 1) * N_TILE)
                        result = work2.tile([M_TILE, N_TILE], F32)
                        if n == 0:
                            nc.scalar.copy(out=result[:], in_=acc[(m, n)][:])
                        else:
                            nc.vector.tensor_copy(out=result[:], in_=acc[(m, n)][:])
                        nc.sync.dma_start(out=out[out_rows, n_cols], in_=result[:])
